import numpy as np
import ml_dtypes


def mxq(x, axis, fmt="e4m3"):
    dtype, down = {"e4m3": (ml_dtypes.float8_e4m3fn, 7), "e5m2": (ml_dtypes.float8_e5m2, 14)}[fmt]
    v = np.moveaxis(np.asarray(x, np.float32).astype(ml_dtypes.bfloat16).astype(np.float64), axis, -1)
    blocks = v.reshape(v.shape[:-1] + (-1, 32))
    amax = np.abs(blocks).max(-1, keepdims=True)
    byte = np.maximum(np.where(amax > 0, np.frexp(amax)[1] - 1 + 127, 0) - down, 1)
    scale = np.exp2(byte - 127.0)
    codes = (blocks / scale).astype(np.float32).astype(dtype).astype(np.float64)
    return np.moveaxis((codes * scale).reshape(v.shape), -1, axis)


WIDE = False


def mx_kscale(k):
    if not WIDE:
        return np.ones(k)
    levels = np.array([10, -10, 5, -5, 0])
    a = np.random.permutation(np.resize(levels, k // 512 * 4)).reshape(k // 512, 4)
    idx = np.arange(k)
    return np.exp2(a[idx // 512, idx % 128 // 32])


BF16 = ml_dtypes.bfloat16


def bf(x):
    return np.asarray(x, np.float32).astype(BF16)


def f64(x):
    return np.asarray(x).astype(np.float64)


E2M1 = np.array([0.0, 0.5, 1.0, 1.5, 2.0, 3.0, 4.0, 6.0, -0.0, -0.5, -1.0, -1.5, -2.0, -3.0, -4.0, -6.0])


def pack_weight(w, fmt):
    k, n = w.shape
    w = f64(bf(w)).reshape(k // 32, 32, n)
    amax = np.abs(w).max(1)
    if fmt == "e4m3":
        byte = np.frexp(amax)[1] - 1 + 127 - 7
    else:
        mant, ex = np.frexp(amax / 6.0)
        byte = np.where(mant > 0.5, ex, ex - 1) + 127
    byte = np.clip(np.where(amax > 0, byte, 1), 1, 254)
    scaled = (w * np.exp2(127.0 - byte)[:, None, :]).reshape(k, n).astype(np.float32)
    by_word = np.ascontiguousarray(scaled.reshape(k // 512, 128, 4, n).transpose(0, 1, 3, 2))
    if fmt == "e4m3":
        words = by_word.astype(ml_dtypes.float8_e4m3fn).view(np.uint8)
    else:
        c = by_word.astype(ml_dtypes.float4_e2m1fn).view(np.uint8) & 0xF
        words = c[..., 0::2] | (c[..., 1::2] << 4)
    return np.ascontiguousarray(words), np.ascontiguousarray(byte.astype(np.uint8).reshape(k // 512, 16, n))


def unpack_weight(words, scales, fmt):
    g, p, n, _ = words.shape
    if fmt == "e4m3":
        vals = np.ascontiguousarray(words).view(ml_dtypes.float8_e4m3fn).astype(np.float64)
    else:
        nib = np.empty((g, p, n, 4), np.uint8)
        nib[..., 0::2] = words & 0xF
        nib[..., 1::2] = words >> 4
        vals = E2M1[nib]
    vals = vals * np.repeat(np.exp2(scales.astype(np.float64) - 127.0), 8, axis=1)[..., None]
    return vals.transpose(0, 1, 3, 2).reshape(g * 512, n)


B, H, W, C, I, O, NH = 1, 2, 512, 512, 512, 512, 8
DH = I // NH
SCALE = DH ** -0.5
FMT = "e4m3"


def setup_inputs():
    s, t = mx_kscale(C), mx_kscale(I)
    sc = s[None, :, None, None]
    left_feat = bf(np.random.standard_normal((B, C, H, W)) * sc)
    right_feat = bf(np.random.standard_normal((B, C, H, W)) * sc)
    wq = np.random.standard_normal((I, C)) / np.sqrt(C) / s[None, :] * t[:, None]
    wk = np.random.standard_normal((I, C)) / np.sqrt(C) / s[None, :] / t[:, None]
    wq_words, wq_scales = pack_weight(np.ascontiguousarray(wq.T), FMT)
    wk_words, wk_scales = pack_weight(np.ascontiguousarray(wk.T), FMT)
    return {"left_feat": left_feat,
            "right_feat": right_feat,
            "wq_words": wq_words, "wq_scales": wq_scales,
            "wk_words": wk_words, "wk_scales": wk_scales}


def reference(left_feat, right_feat, wq_words, wq_scales, wk_words, wk_scales):
    lf = f64(left_feat).reshape(B, C, H * W)
    rf = f64(right_feat).reshape(B, C, H * W)
    q = unpack_weight(wq_words, wq_scales, FMT).T @ mxq(lf, 1, "e4m3")
    k = unpack_weight(wk_words, wk_scales, FMT).T @ mxq(rf, 1, "e4m3")
    q = q.reshape(B, I, H, W).transpose(0, 2, 3, 1)
    k = k.reshape(B, I, H, W).transpose(0, 2, 1, 3)
    return (mxq(q, 3, "e4m3") @ mxq(k, 2, "e4m3")) * SCALE

@@ -1,0 +1,180 @@
+from contextlib import ExitStack
+
+import concourse.mybir as mybir
+
+F32 = mybir.dt.float32
+BF16 = mybir.dt.bfloat16
+I32 = mybir.dt.int32
+U32 = mybir.dt.uint32
+U8 = mybir.dt.uint8
+FP8X4 = mybir.dt.float8_e4m3fn_x4
+
+P = 128
+PACK = 4
+C = 512
+O = 512
+H = 2
+W = 512
+SCALE = 0.125
+
+CHUNK = 128
+PIECE = 256
+CHUNKS_IN_PIECE = PIECE // CHUNK
+PIECES_IN_ROW = W // PIECE
+
+PROJECT_LAG = 1
+REQUANTISE_LAG = 4
+STORE_LAG = 6
+
+FLOPS = 2 * (2 * C * O * H * W) + 2 * H * W * W * O
+
+
+def tile_sttm_single_pa_kernel(
+    tc, left_feat, right_feat, wq_words, wq_scales, wk_words, wk_scales, out
+):
+    nc = tc.nc
+    features = {"q": left_feat, "k": right_feat}
+    weights = {"q": (wq_words, wq_scales), "k": (wk_words, wk_scales)}
+
+    row_sides = [(h, side) for h in range(H) for side in ("k", "q")]
+    pieces = [(h, side, i) for (h, side) in row_sides for i in range(PIECES_IN_ROW)]
+
+    with ExitStack() as ctx:
+        keep = ctx.enter_context(tc.tile_pool(name="keep", bufs=1))
+        psum = ctx.enter_context(tc.psum_pool(name="psum", bufs=4))
+        ctx.enter_context(tc.manual_schedule())
+
+        w_codes = {}
+        w_plane = {}
+        for side in ("k", "q"):
+            w_codes[side] = keep.tile([P, O], U32, name="w_codes_" + side, align_bytes=64)
+            w_plane[side] = keep.tile([P, O], U8, name="w_plane_" + side, align_bytes=64)
+        raw = {}
+        grouped = {}
+        x_codes = {}
+        x_plane = {}
+        y_grouped = {}
+        y_codes = {}
+        y_plane = {}
+        for (h, side) in row_sides:
+            tail = "_%s%d" % (side, h)
+            raw[h, side] = keep.tile([P, PACK, W], BF16, name="raw" + tail)
+            grouped[h, side] = keep.tile([P, W, PACK], BF16, name="grouped" + tail, align_bytes=64)
+            x_codes[h, side] = keep.tile([P, W], U32, name="x_codes" + tail, align_bytes=64)
+            x_plane[h, side] = keep.tile([P, W], U8, name="x_plane" + tail, align_bytes=64)
+            y_grouped[h, side] = keep.tile([P, W, PACK], BF16, name="y_grouped" + tail, align_bytes=64)
+            y_codes[h, side] = keep.tile([P, W], U32, name="y_codes" + tail, align_bytes=64)
+            y_plane[h, side] = keep.tile([P, W], U8, name="y_plane" + tail, align_bytes=64)
+        product_banks = {}
+
+        def load_features(h, side):
+            rows = features[side][0].rearrange("(p j) h w -> p j h w", j=PACK)
+            nc.sync.dma_start(out=raw[h, side][:], in_=rows[:, :, h, :])
+
+        def load_weight(side):
+            words, scales = weights[side]
+            plane_words = w_plane[side][:].bitcast(I32)
+            scale_rows = scales[0].bitcast(I32).rearrange("(quad r) n -> r quad n", r=4)
+            for r in range(4):
+                nc.sync.dma_start(out=plane_words[r:P:32, :], in_=scale_rows[r])
+            nc.sync.dma_start(
+                out=w_codes[side][:].bitcast(I32),
+                in_=words[0].rearrange("p n t -> p (n t)").bitcast(I32),
+            )
+
+        def regroup(h, side, i):
+            cols = slice(i * PIECE, (i + 1) * PIECE)
+            nc.vector.tensor_copy(
+                out=grouped[h, side][:, cols, :].rearrange("p (c r) j -> p c j r", r=4),
+                in_=raw[h, side][:, :, cols].rearrange("p j (c r) -> p c j r", r=4),
+            )
+
+        def quantise(codes, plane, values, cols):
+            nc.vector.quantize_mx(
+                out=codes[:, cols].bitcast(FP8X4),
+                scales=plane[:, cols],
+                in_=values[:, cols, :].rearrange("p w j -> p (w j)"),
+            )
+
+        def project(h, side, i):
+            for chunk in range(i * CHUNKS_IN_PIECE, (i + 1) * CHUNKS_IN_PIECE):
+                cols = slice(chunk * CHUNK, (chunk + 1) * CHUNK)
+                bank = psum.tile([P, PACK, CHUNK], F32, name="projection", tag="projection")
+                for t in range(PACK):
+                    o_cols = slice(t * P, (t + 1) * P)
+                    nc.tensor.matmul_mx(
+                        out=bank[:, t, :],
+                        lhsT=w_codes[side][:, o_cols].bitcast(FP8X4),
+                        lhsT_scale=w_plane[side][:, o_cols],
+                        rhs=x_codes[h, side][:, cols].bitcast(FP8X4),
+                        rhs_scale=x_plane[h, side][:, cols],
+                        start=True,
+                        stop=True,
+                    )
+                nc.scalar.copy(
+                    out=y_grouped[h, side][:, cols, :],
+                    in_=bank[:].rearrange("p t w -> p w t"),
+                )
+
+        def multiply(h, i):
+            for chunk in range(i * CHUNKS_IN_PIECE, (i + 1) * CHUNKS_IN_PIECE):
+                cols = slice(chunk * CHUNK, (chunk + 1) * CHUNK)
+                bank = psum.tile([P, W], F32, name="product", tag="product")
+                nc.tensor.matmul_mx(
+                    out=bank[:],
+                    lhsT=y_codes[h, "q"][:, cols].bitcast(FP8X4),
+                    lhsT_scale=y_plane[h, "q"][:, cols],
+                    rhs=y_codes[h, "k"][:].bitcast(FP8X4),
+                    rhs_scale=y_plane[h, "k"][:],
+                    start=True,
+                    stop=True,
+                )
+                product_banks[h, chunk] = bank
+
+        def scale_and_store(h, i):
+            for chunk in range(i * CHUNKS_IN_PIECE, (i + 1) * CHUNKS_IN_PIECE):
+                scores = keep.tile([P, W], F32, name="scores_%d_%d" % (h, chunk))
+                if chunk % 2 == 0:
+                    nc.scalar.mul(out=scores[:], in_=product_banks[h, chunk][:], mul=SCALE)
+                else:
+                    nc.vector.tensor_scalar_mul(
+                        out=scores[:], in0=product_banks[h, chunk][:], scalar1=SCALE
+                    )
+                nc.sync.dma_start(
+                    out=out[0, h, chunk * CHUNK : (chunk + 1) * CHUNK, :], in_=scores[:]
+                )
+
+        for side in ("k", "q"):
+            nc.vector.memset(w_plane[side][:].bitcast(I32), 0)
+        warm = keep.tile([P, 1], F32, name="warm")
+        nc.vector.memset(warm[:], 0.0)
+        nc.scalar.mul(out=warm[:], in_=warm[:], mul=SCALE)
+
+        load_features(0, "k")
+        load_weight("k")
+        load_features(0, "q")
+        load_weight("q")
+        load_features(1, "k")
+        load_features(1, "q")
+
+        def piece_at(step):
+            return pieces[step] if 0 <= step < len(pieces) else None
+
+        for s in range(len(pieces) + STORE_LAG):
+            if piece_at(s):
+                regroup(*piece_at(s))
+            if piece_at(s - PROJECT_LAG):
+                h, side, i = piece_at(s - PROJECT_LAG)
+                cols = slice(i * PIECE, (i + 1) * PIECE)
+                quantise(x_codes[h, side], x_plane[h, side], grouped[h, side], cols)
+                project(h, side, i)
+            if piece_at(s - REQUANTISE_LAG):
+                h, side, i = piece_at(s - REQUANTISE_LAG)
+                cols = slice(i * PIECE, (i + 1) * PIECE)
+                quantise(y_codes[h, side], y_plane[h, side], y_grouped[h, side], cols)
+                if side == "q":
+                    multiply(h, i)
+            if piece_at(s - STORE_LAG):
+                h, side, i = piece_at(s - STORE_LAG)
+                if side == "q":
+                    scale_and_store(h, i)

@@ -21,10 +21,11 @@ CHUNK = 128
 PIECE = 256
 CHUNKS_IN_PIECE = PIECE // CHUNK
 PIECES_IN_ROW = W // PIECE
+CHUNKS_IN_ROW = W // CHUNK
 
 PROJECT_LAG = 1
 REQUANTISE_LAG = 4
-STORE_LAG = 6
+STORE_LAG = 7
 
 FLOPS = 2 * (2 * C * O * H * W) + 2 * H * W * W * O
 
@@ -134,7 +135,7 @@ def tile_sttm_single_pa_kernel(
         def scale_and_store(h, i):
             for chunk in range(i * CHUNKS_IN_PIECE, (i + 1) * CHUNKS_IN_PIECE):
                 scores = keep.tile([P, W], F32, name="scores_%d_%d" % (h, chunk))
-                if chunk % 2 == 0:
+                if chunk == CHUNKS_IN_ROW - 1:
                     nc.scalar.mul(out=scores[:], in_=product_banks[h, chunk][:], mul=SCALE)
                 else:
                     nc.vector.tensor_scalar_mul(

@@ -147,9 +147,6 @@ def tile_sttm_single_pa_kernel(
 
         for side in ("k", "q"):
             nc.vector.memset(w_plane[side][:].bitcast(I32), 0)
-        warm = keep.tile([P, 1], F32, name="warm")
-        nc.vector.memset(warm[:], 0.0)
-        nc.scalar.mul(out=warm[:], in_=warm[:], mul=SCALE)
 
         load_features(0, "k")
         load_weight("k")

@@ -18,14 +18,6 @@ W = 512
 SCALE = 0.125
 
 CHUNK = 128
-PIECE = 256
-CHUNKS_IN_PIECE = PIECE // CHUNK
-PIECES_IN_ROW = W // PIECE
-CHUNKS_IN_ROW = W // CHUNK
-
-PROJECT_LAG = 1
-REQUANTISE_LAG = 4
-STORE_LAG = 7
 
 FLOPS = 2 * (2 * C * O * H * W) + 2 * H * W * W * O
 
@@ -36,15 +28,12 @@ def tile_sttm_single_pa_kernel(
     nc = tc.nc
     features = {"q": left_feat, "k": right_feat}
     weights = {"q": (wq_words, wq_scales), "k": (wk_words, wk_scales)}
-
     row_sides = [(h, side) for h in range(H) for side in ("k", "q")]
-    pieces = [(h, side, i) for (h, side) in row_sides for i in range(PIECES_IN_ROW)]
 
     with ExitStack() as ctx:
         keep = ctx.enter_context(tc.tile_pool(name="keep", bufs=1))
         psum = ctx.enter_context(tc.psum_pool(name="psum", bufs=4))
         ctx.enter_context(tc.manual_schedule())
-
         w_codes = {}
         w_plane = {}
         for side in ("k", "q"):
@@ -67,39 +56,46 @@ def tile_sttm_single_pa_kernel(
             y_codes[h, side] = keep.tile([P, W], U32, name="y_codes" + tail, align_bytes=64)
             y_plane[h, side] = keep.tile([P, W], U8, name="y_plane" + tail, align_bytes=64)
         product_banks = {}
+        projection_banks = {}
 
-        def load_features(h, side):
+
+        def load_features(queue, h, side, a, b):
             rows = features[side][0].rearrange("(p j) h w -> p j h w", j=PACK)
-            nc.sync.dma_start(out=raw[h, side][:], in_=rows[:, :, h, :])
+            queue.dma_start(out=raw[h, side][:, :, a:b], in_=rows[:, :, h, a:b])
 
-        def load_weight(side):
-            words, scales = weights[side]
+        def load_scales(side):
             plane_words = w_plane[side][:].bitcast(I32)
-            scale_rows = scales[0].bitcast(I32).rearrange("(quad r) n -> r quad n", r=4)
+            scale_rows = weights[side][1][0].bitcast(I32).rearrange("(quad r) n -> r quad n", r=4)
             for r in range(4):
                 nc.sync.dma_start(out=plane_words[r:P:32, :], in_=scale_rows[r])
+
+        def load_words(side):
             nc.sync.dma_start(
                 out=w_codes[side][:].bitcast(I32),
-                in_=words[0].rearrange("p n t -> p (n t)").bitcast(I32),
+                in_=weights[side][0][0].rearrange("p n t -> p (n t)").bitcast(I32),
             )
 
-        def regroup(h, side, i):
-            cols = slice(i * PIECE, (i + 1) * PIECE)
-            nc.vector.tensor_copy(
-                out=grouped[h, side][:, cols, :].rearrange("p (c r) j -> p c j r", r=4),
-                in_=raw[h, side][:, :, cols].rearrange("p j (c r) -> p c j r", r=4),
+        def regroup(copy, h, side, a, b):
+            copy(
+                out=grouped[h, side][:, a:b, :].rearrange("p (c r) j -> p c j r", r=4),
+                in_=raw[h, side][:, :, a:b].rearrange("p j (c r) -> p c j r", r=4),
             )
 
-        def quantise(codes, plane, values, cols):
+        def quantise(codes, plane, values, a, b):
             nc.vector.quantize_mx(
-                out=codes[:, cols].bitcast(FP8X4),
-                scales=plane[:, cols],
-                in_=values[:, cols, :].rearrange("p w j -> p (w j)"),
+                out=codes[:, a:b].bitcast(FP8X4),
+                scales=plane[:, a:b],
+                in_=values[:, a:b, :].rearrange("p w j -> p (w j)"),
             )
 
-        def project(h, side, i):
-            for chunk in range(i * CHUNKS_IN_PIECE, (i + 1) * CHUNKS_IN_PIECE):
-                cols = slice(chunk * CHUNK, (chunk + 1) * CHUNK)
+        def quantise_features(h, side, a, b):
+            quantise(x_codes[h, side], x_plane[h, side], grouped[h, side], a, b)
+
+        def quantise_projection(h, side, a, b):
+            quantise(y_codes[h, side], y_plane[h, side], y_grouped[h, side], a, b)
+
+        def project(h, side, a, b):
+            for start in range(a, b, CHUNK):
                 bank = psum.tile([P, PACK, CHUNK], F32, name="projection", tag="projection")
                 for t in range(PACK):
                     o_cols = slice(t * P, (t + 1) * P)
@@ -107,72 +103,112 @@ def tile_sttm_single_pa_kernel(
                         out=bank[:, t, :],
                         lhsT=w_codes[side][:, o_cols].bitcast(FP8X4),
                         lhsT_scale=w_plane[side][:, o_cols],
-                        rhs=x_codes[h, side][:, cols].bitcast(FP8X4),
-                        rhs_scale=x_plane[h, side][:, cols],
+                        rhs=x_codes[h, side][:, start : start + CHUNK].bitcast(FP8X4),
+                        rhs_scale=x_plane[h, side][:, start : start + CHUNK],
                         start=True,
                         stop=True,
                     )
-                nc.scalar.copy(
-                    out=y_grouped[h, side][:, cols, :],
-                    in_=bank[:].rearrange("p t w -> p w t"),
+                projection_banks[h, side, start] = bank
+
+        def round_projection(copy, h, side, a, b):
+            for start in range(a, b, CHUNK):
+                copy(
+                    out=y_grouped[h, side][:, start : start + CHUNK, :],
+                    in_=projection_banks[h, side, start][:].rearrange("p t w -> p w t"),
                 )
 
-        def multiply(h, i):
-            for chunk in range(i * CHUNKS_IN_PIECE, (i + 1) * CHUNKS_IN_PIECE):
-                cols = slice(chunk * CHUNK, (chunk + 1) * CHUNK)
+        def multiply(h, a, b):
+            for start in range(a, b, CHUNK):
                 bank = psum.tile([P, W], F32, name="product", tag="product")
                 nc.tensor.matmul_mx(
                     out=bank[:],
-                    lhsT=y_codes[h, "q"][:, cols].bitcast(FP8X4),
-                    lhsT_scale=y_plane[h, "q"][:, cols],
+                    lhsT=y_codes[h, "q"][:, start : start + CHUNK].bitcast(FP8X4),
+                    lhsT_scale=y_plane[h, "q"][:, start : start + CHUNK],
                     rhs=y_codes[h, "k"][:].bitcast(FP8X4),
                     rhs_scale=y_plane[h, "k"][:],
                     start=True,
                     stop=True,
                 )
-                product_banks[h, chunk] = bank
+                product_banks[h, start] = bank
 
-        def scale_and_store(h, i):
-            for chunk in range(i * CHUNKS_IN_PIECE, (i + 1) * CHUNKS_IN_PIECE):
-                scores = keep.tile([P, W], F32, name="scores_%d_%d" % (h, chunk))
-                if chunk == CHUNKS_IN_ROW - 1:
-                    nc.scalar.mul(out=scores[:], in_=product_banks[h, chunk][:], mul=SCALE)
+        def scale_and_store(engine, h, a, b):
+            for start in range(a, b, CHUNK):
+                scores = keep.tile([P, W], F32, name="scores_%d_%d" % (h, start))
+                if engine == "S":
+                    nc.scalar.mul(out=scores[:], in_=product_banks[h, start][:], mul=SCALE)
                 else:
                     nc.vector.tensor_scalar_mul(
-                        out=scores[:], in0=product_banks[h, chunk][:], scalar1=SCALE
+                        out=scores[:], in0=product_banks[h, start][:], scalar1=SCALE
                     )
-                nc.sync.dma_start(
-                    out=out[0, h, chunk * CHUNK : (chunk + 1) * CHUNK, :], in_=scores[:]
-                )
+                nc.sync.dma_start(out=out[0, h, start : start + CHUNK, :], in_=scores[:])
 
         for side in ("k", "q"):
             nc.vector.memset(w_plane[side][:].bitcast(I32), 0)
 
-        load_features(0, "k")
-        load_weight("k")
-        load_features(0, "q")
-        load_weight("q")
-        load_features(1, "k")
-        load_features(1, "q")
+        load_features(nc.sync, 0, "k", 0, 256)
+        load_features(nc.sync, 0, "k", 256, 512)
+        load_scales("k")
+        load_words("k")
+        load_features(nc.sync, 0, "q", 0, 256)
+        load_features(nc.sync, 0, "q", 256, 512)
+        load_scales("q")
+        load_words("q")
+        load_features(nc.sync, 1, "k", 0, 512)
+        load_features(nc.sync, 1, "q", 0, 512)
 
-        def piece_at(step):
-            return pieces[step] if 0 <= step < len(pieces) else None
-
-        for s in range(len(pieces) + STORE_LAG):
-            if piece_at(s):
-                regroup(*piece_at(s))
-            if piece_at(s - PROJECT_LAG):
-                h, side, i = piece_at(s - PROJECT_LAG)
-                cols = slice(i * PIECE, (i + 1) * PIECE)
-                quantise(x_codes[h, side], x_plane[h, side], grouped[h, side], cols)
-                project(h, side, i)
-            if piece_at(s - REQUANTISE_LAG):
-                h, side, i = piece_at(s - REQUANTISE_LAG)
-                cols = slice(i * PIECE, (i + 1) * PIECE)
-                quantise(y_codes[h, side], y_plane[h, side], y_grouped[h, side], cols)
-                if side == "q":
-                    multiply(h, i)
-            if piece_at(s - STORE_LAG):
-                h, side, i = piece_at(s - STORE_LAG)
-                if side == "q":
-                    scale_and_store(h, i)
+        regroup(nc.vector.tensor_copy, 0, "k", 0, 128)
+        regroup(nc.scalar.copy, 0, "k", 128, 256)
+        regroup(nc.vector.tensor_copy, 0, "k", 256, 384)
+        regroup(nc.scalar.copy, 0, "k", 384, 512)
+        quantise_features(0, "k", 0, 256)
+        project(0, "k", 0, 256)
+        round_projection(nc.scalar.copy, 0, "k", 0, 256)
+        quantise_features(0, "k", 256, 512)
+        project(0, "k", 256, 512)
+        round_projection(nc.scalar.copy, 0, "k", 256, 512)
+        regroup(nc.vector.tensor_copy, 0, "q", 0, 256)
+        regroup(nc.vector.tensor_copy, 0, "q", 256, 512)
+        quantise_features(0, "q", 0, 256)
+        project(0, "q", 0, 256)
+        round_projection(nc.scalar.copy, 0, "q", 0, 256)
+        quantise_features(0, "q", 256, 512)
+        project(0, "q", 256, 512)
+        round_projection(nc.scalar.copy, 0, "q", 256, 512)
+        quantise_projection(0, "k", 0, 256)
+        regroup(nc.vector.tensor_copy, 1, "k", 0, 256)
+        regroup(nc.vector.tensor_copy, 1, "k", 256, 512)
+        quantise_features(1, "k", 0, 256)
+        project(1, "k", 0, 256)
+        round_projection(nc.scalar.copy, 1, "k", 0, 256)
+        quantise_projection(0, "k", 256, 512)
+        quantise_projection(0, "q", 0, 256)
+        multiply(0, 0, 256)
+        quantise_features(1, "k", 256, 512)
+        project(1, "k", 256, 512)
+        scale_and_store("S", 0, 0, 128)
+        regroup(nc.vector.tensor_copy, 1, "q", 0, 256)
+        quantise_features(1, "q", 0, 256)
+        project(1, "q", 0, 256)
+        round_projection(nc.scalar.copy, 1, "k", 256, 384)
+        quantise_projection(0, "q", 256, 512)
+        multiply(0, 256, 512)
+        regroup(nc.vector.tensor_copy, 1, "q", 256, 512)
+        quantise_features(1, "q", 256, 512)
+        scale_and_store("S", 0, 128, 256)
+        round_projection(nc.vector.tensor_copy, 1, "k", 384, 512)
+        round_projection(nc.scalar.copy, 1, "q", 0, 256)
+        project(1, "q", 256, 512)
+        quantise_projection(1, "k", 0, 256)
+        quantise_projection(1, "k", 256, 512)
+        scale_and_store("S", 0, 256, 384)
+        round_projection(nc.scalar.copy, 1, "q", 256, 384)
+        quantise_projection(1, "q", 0, 256)
+        multiply(1, 0, 256)
+        round_projection(nc.vector.tensor_copy, 1, "q", 384, 512)
+        scale_and_store("S", 0, 384, 512)
+        quantise_projection(1, "q", 256, 512)
+        multiply(1, 256, 512)
+        scale_and_store("S", 1, 0, 128)
+        scale_and_store("V", 1, 128, 256)
+        scale_and_store("S", 1, 256, 384)
+        scale_and_store("V", 1, 384, 512)

@@ -117,36 +117,35 @@ def tile_sttm_single_pa_kernel(
                     in_=projection_banks[h, side, start][:].rearrange("p t w -> p w t"),
                 )
 
-        def multiply(h, a, b):
+        def multiply(h, a, b, x0=0, x1=W):
             for start in range(a, b, CHUNK):
-                bank = psum.tile([P, W], F32, name="product", tag="product")
+                bank = psum.tile([P, x1 - x0], F32, name="product", tag="product")
                 nc.tensor.matmul_mx(
                     out=bank[:],
                     lhsT=y_codes[h, "q"][:, start : start + CHUNK].bitcast(FP8X4),
                     lhsT_scale=y_plane[h, "q"][:, start : start + CHUNK],
-                    rhs=y_codes[h, "k"][:].bitcast(FP8X4),
-                    rhs_scale=y_plane[h, "k"][:],
+                    rhs=y_codes[h, "k"][:, x0:x1].bitcast(FP8X4),
+                    rhs_scale=y_plane[h, "k"][:, x0:x1],
                     start=True,
                     stop=True,
                 )
-                product_banks[h, start] = bank
+                product_banks[h, start, x0] = bank
 
-        def scale_and_store(engine, h, a, b):
+        def scale_and_store(engine, h, a, b, x0=0, x1=W):
             for start in range(a, b, CHUNK):
-                scores = keep.tile([P, W], F32, name="scores_%d_%d" % (h, start))
+                scores = keep.tile([P, x1 - x0], F32, name="scores_%d_%d_%d" % (h, start, x0))
+                bank = product_banks[h, start, x0]
                 if engine == "S":
-                    nc.scalar.mul(out=scores[:], in_=product_banks[h, start][:], mul=SCALE)
+                    nc.scalar.mul(out=scores[:], in_=bank[:], mul=SCALE)
                 else:
-                    nc.vector.tensor_scalar_mul(
-                        out=scores[:], in0=product_banks[h, start][:], scalar1=SCALE
-                    )
-                nc.sync.dma_start(out=out[0, h, start : start + CHUNK, :], in_=scores[:])
+                    nc.vector.tensor_scalar_mul(out=scores[:], in0=bank[:], scalar1=SCALE)
+                nc.sync.dma_start(out=out[0, h, start : start + CHUNK, x0:x1], in_=scores[:])
 
         for side in ("k", "q"):
             nc.vector.memset(w_plane[side][:].bitcast(I32), 0)
 
-        load_features(nc.sync, 0, "k", 0, 256)
-        load_features(nc.sync, 0, "k", 256, 512)
+        load_features(nc.scalar, 0, "k", 0, 256)
+        load_features(nc.scalar, 0, "k", 256, 512)
         load_scales("k")
         load_words("k")
         load_features(nc.sync, 0, "q", 0, 256)
@@ -156,13 +155,12 @@ def tile_sttm_single_pa_kernel(
         load_features(nc.sync, 1, "k", 0, 512)
         load_features(nc.sync, 1, "q", 0, 512)
 
-        regroup(nc.vector.tensor_copy, 0, "k", 0, 128)
-        regroup(nc.scalar.copy, 0, "k", 128, 256)
-        regroup(nc.vector.tensor_copy, 0, "k", 256, 384)
-        regroup(nc.scalar.copy, 0, "k", 384, 512)
+        regroup(nc.vector.tensor_copy, 0, "k", 0, 256)
+        regroup(nc.scalar.copy, 0, "k", 256, 384)
         quantise_features(0, "k", 0, 256)
         project(0, "k", 0, 256)
         round_projection(nc.scalar.copy, 0, "k", 0, 256)
+        regroup(nc.vector.tensor_copy, 0, "k", 384, 512)
         quantise_features(0, "k", 256, 512)
         project(0, "k", 256, 512)
         round_projection(nc.scalar.copy, 0, "k", 256, 512)
@@ -180,35 +178,38 @@ def tile_sttm_single_pa_kernel(
         quantise_features(1, "k", 0, 256)
         project(1, "k", 0, 256)
         round_projection(nc.scalar.copy, 1, "k", 0, 256)
+        quantise_features(1, "k", 256, 512)
+        project(1, "k", 256, 512)
         quantise_projection(0, "k", 256, 512)
         quantise_projection(0, "q", 0, 256)
         multiply(0, 0, 256)
-        quantise_features(1, "k", 256, 512)
-        project(1, "k", 256, 512)
-        scale_and_store("S", 0, 0, 128)
+        scale_and_store("S", 0, 0, 256)
         regroup(nc.vector.tensor_copy, 1, "q", 0, 256)
-        quantise_features(1, "q", 0, 256)
-        project(1, "q", 0, 256)
-        round_projection(nc.scalar.copy, 1, "k", 256, 384)
         quantise_projection(0, "q", 256, 512)
         multiply(0, 256, 512)
+        quantise_features(1, "q", 0, 256)
+        project(1, "q", 0, 256)
         regroup(nc.vector.tensor_copy, 1, "q", 256, 512)
-        quantise_features(1, "q", 256, 512)
-        scale_and_store("S", 0, 128, 256)
-        round_projection(nc.vector.tensor_copy, 1, "k", 384, 512)
-        round_projection(nc.scalar.copy, 1, "q", 0, 256)
-        project(1, "q", 256, 512)
+        round_projection(nc.vector.tensor_copy, 1, "k", 256, 384)
+        round_projection(nc.scalar.copy, 1, "k", 384, 512)
         quantise_projection(1, "k", 0, 256)
-        quantise_projection(1, "k", 256, 512)
+        quantise_features(1, "q", 256, 512)
+        project(1, "q", 256, 512)
+        round_projection(nc.scalar.copy, 1, "q", 0, 128)
+        round_projection(nc.vector.tensor_copy, 1, "q", 128, 256)
         scale_and_store("S", 0, 256, 384)
-        round_projection(nc.scalar.copy, 1, "q", 256, 384)
+        quantise_projection(1, "k", 256, 512)
         quantise_projection(1, "q", 0, 256)
         multiply(1, 0, 256)
-        round_projection(nc.vector.tensor_copy, 1, "q", 384, 512)
-        scale_and_store("S", 0, 384, 512)
-        quantise_projection(1, "q", 256, 512)
-        multiply(1, 256, 512)
-        scale_and_store("S", 1, 0, 128)
-        scale_and_store("V", 1, 128, 256)
+        round_projection(nc.scalar.copy, 1, "q", 256, 512)
+        scale_and_store("V", 0, 384, 512)
+        quantise_projection(1, "q", 256, 384)
+        multiply(1, 256, 384)
+        scale_and_store("V", 1, 0, 128)
+        quantise_projection(1, "q", 384, 512)
+        scale_and_store("S", 1, 128, 256)
+        multiply(1, 384, 512, 0, 256)
+        multiply(1, 384, 512, 256, 512)
         scale_and_store("S", 1, 256, 384)
-        scale_and_store("V", 1, 384, 512)
+        scale_and_store("V", 1, 384, 512, 0, 256)
+        scale_and_store("V", 1, 384, 512, 256, 512)

@@ -155,15 +155,22 @@ def tile_sttm_single_pa_kernel(
         load_features(nc.sync, 1, "k", 0, 512)
         load_features(nc.sync, 1, "q", 0, 512)
 
-        regroup(nc.vector.tensor_copy, 0, "k", 0, 256)
-        regroup(nc.scalar.copy, 0, "k", 256, 384)
-        quantise_features(0, "k", 0, 256)
-        project(0, "k", 0, 256)
-        round_projection(nc.scalar.copy, 0, "k", 0, 256)
+        regroup(nc.vector.tensor_copy, 0, "k", 0, 128)
+        regroup(nc.vector.tensor_copy, 0, "k", 128, 256)
+        quantise_features(0, "k", 0, 128)
+        project(0, "k", 0, 128)
+        round_projection(nc.scalar.copy, 0, "k", 0, 128)
+        quantise_features(0, "k", 128, 256)
+        project(0, "k", 128, 256)
+        round_projection(nc.scalar.copy, 0, "k", 128, 256)
+        regroup(nc.vector.tensor_copy, 0, "k", 256, 384)
         regroup(nc.vector.tensor_copy, 0, "k", 384, 512)
-        quantise_features(0, "k", 256, 512)
-        project(0, "k", 256, 512)
-        round_projection(nc.scalar.copy, 0, "k", 256, 512)
+        quantise_features(0, "k", 256, 384)
+        project(0, "k", 256, 384)
+        round_projection(nc.scalar.copy, 0, "k", 256, 384)
+        quantise_features(0, "k", 384, 512)
+        project(0, "k", 384, 512)
+        round_projection(nc.scalar.copy, 0, "k", 384, 512)
         regroup(nc.vector.tensor_copy, 0, "q", 0, 256)
         regroup(nc.vector.tensor_copy, 0, "q", 256, 512)
         quantise_features(0, "q", 0, 256)

@@ -148,8 +148,7 @@ def tile_sttm_single_pa_kernel(
         load_features(nc.scalar, 0, "k", 256, 512)
         load_scales("k")
         load_words("k")
-        load_features(nc.sync, 0, "q", 0, 256)
-        load_features(nc.sync, 0, "q", 256, 512)
+        load_features(nc.sync, 0, "q", 0, 512)
         load_scales("q")
         load_words("q")
         load_features(nc.sync, 1, "k", 0, 512)

@@ -218,4 +218,4 @@ def tile_sttm_single_pa_kernel(
         multiply(1, 384, 512, 256, 512)
         scale_and_store("S", 1, 256, 384)
         scale_and_store("V", 1, 384, 512, 0, 256)
-        scale_and_store("V", 1, 384, 512, 256, 512)
+        scale_and_store("S", 1, 384, 512, 256, 512)

from contextlib import ExitStack

import concourse.mybir as mybir

F32 = mybir.dt.float32
BF16 = mybir.dt.bfloat16
I32 = mybir.dt.int32
U32 = mybir.dt.uint32
U8 = mybir.dt.uint8
FP8X4 = mybir.dt.float8_e4m3fn_x4

P = 128
PACK = 4
C = 512
O = 512
H = 2
W = 512
SCALE = 0.125

CHUNK = 128

FLOPS = 2 * (2 * C * O * H * W) + 2 * H * W * W * O


def tile_sttm_single_pa_kernel(
    tc, left_feat, right_feat, wq_words, wq_scales, wk_words, wk_scales, out
):
    nc = tc.nc
    features = {"q": left_feat, "k": right_feat}
    weights = {"q": (wq_words, wq_scales), "k": (wk_words, wk_scales)}
    row_sides = [(h, side) for h in range(H) for side in ("k", "q")]

    with ExitStack() as ctx:
        keep = ctx.enter_context(tc.tile_pool(name="keep", bufs=1))
        psum = ctx.enter_context(tc.psum_pool(name="psum", bufs=4))
        ctx.enter_context(tc.manual_schedule())
        w_codes = {}
        w_plane = {}
        for side in ("k", "q"):
            w_codes[side] = keep.tile([P, O], U32, name="w_codes_" + side, align_bytes=64)
            w_plane[side] = keep.tile([P, O], U8, name="w_plane_" + side, align_bytes=64)
        raw = {}
        grouped = {}
        x_codes = {}
        x_plane = {}
        y_grouped = {}
        y_codes = {}
        y_plane = {}
        for (h, side) in row_sides:
            tail = "_%s%d" % (side, h)
            raw[h, side] = keep.tile([P, PACK, W], BF16, name="raw" + tail)
            grouped[h, side] = keep.tile([P, W, PACK], BF16, name="grouped" + tail, align_bytes=64)
            x_codes[h, side] = keep.tile([P, W], U32, name="x_codes" + tail, align_bytes=64)
            x_plane[h, side] = keep.tile([P, W], U8, name="x_plane" + tail, align_bytes=64)
            y_grouped[h, side] = keep.tile([P, W, PACK], BF16, name="y_grouped" + tail, align_bytes=64)
            y_codes[h, side] = keep.tile([P, W], U32, name="y_codes" + tail, align_bytes=64)
            y_plane[h, side] = keep.tile([P, W], U8, name="y_plane" + tail, align_bytes=64)
        product_banks = {}
        projection_banks = {}


        def load_features(queue, h, side, a, b):
            rows = features[side][0].rearrange("(p j) h w -> p j h w", j=PACK)
            queue.dma_start(out=raw[h, side][:, :, a:b], in_=rows[:, :, h, a:b])

        def load_scales(side):
            plane_words = w_plane[side][:].bitcast(I32)
            scale_rows = weights[side][1][0].bitcast(I32).rearrange("(quad r) n -> r quad n", r=4)
            for r in range(4):
                nc.sync.dma_start(out=plane_words[r:P:32, :], in_=scale_rows[r])

        def load_words(side):
            nc.sync.dma_start(
                out=w_codes[side][:].bitcast(I32),
                in_=weights[side][0][0].rearrange("p n t -> p (n t)").bitcast(I32),
            )

        def regroup(copy, h, side, a, b):
            copy(
                out=grouped[h, side][:, a:b, :].rearrange("p (c r) j -> p c j r", r=4),
                in_=raw[h, side][:, :, a:b].rearrange("p j (c r) -> p c j r", r=4),
            )

        def quantise(codes, plane, values, a, b):
            nc.vector.quantize_mx(
                out=codes[:, a:b].bitcast(FP8X4),
                scales=plane[:, a:b],
                in_=values[:, a:b, :].rearrange("p w j -> p (w j)"),
            )

        def quantise_features(h, side, a, b):
            quantise(x_codes[h, side], x_plane[h, side], grouped[h, side], a, b)

        def quantise_projection(h, side, a, b):
            quantise(y_codes[h, side], y_plane[h, side], y_grouped[h, side], a, b)

        def project(h, side, a, b):
            for start in range(a, b, CHUNK):
                bank = psum.tile([P, PACK, CHUNK], F32, name="projection", tag="projection")
                for t in range(PACK):
                    o_cols = slice(t * P, (t + 1) * P)
                    nc.tensor.matmul_mx(
                        out=bank[:, t, :],
                        lhsT=w_codes[side][:, o_cols].bitcast(FP8X4),
                        lhsT_scale=w_plane[side][:, o_cols],
                        rhs=x_codes[h, side][:, start : start + CHUNK].bitcast(FP8X4),
                        rhs_scale=x_plane[h, side][:, start : start + CHUNK],
                        start=True,
                        stop=True,
                    )
                projection_banks[h, side, start] = bank

        def round_projection(copy, h, side, a, b):
            for start in range(a, b, CHUNK):
                copy(
                    out=y_grouped[h, side][:, start : start + CHUNK, :],
                    in_=projection_banks[h, side, start][:].rearrange("p t w -> p w t"),
                )

        def multiply(h, a, b, x0=0, x1=W):
            for start in range(a, b, CHUNK):
                bank = psum.tile([P, x1 - x0], F32, name="product", tag="product")
                nc.tensor.matmul_mx(
                    out=bank[:],
                    lhsT=y_codes[h, "q"][:, start : start + CHUNK].bitcast(FP8X4),
                    lhsT_scale=y_plane[h, "q"][:, start : start + CHUNK],
                    rhs=y_codes[h, "k"][:, x0:x1].bitcast(FP8X4),
                    rhs_scale=y_plane[h, "k"][:, x0:x1],
                    start=True,
                    stop=True,
                )
                product_banks[h, start, x0] = bank

        def scale_and_store(engine, h, a, b, x0=0, x1=W):
            for start in range(a, b, CHUNK):
                scores = keep.tile([P, x1 - x0], F32, name="scores_%d_%d_%d" % (h, start, x0))
                bank = product_banks[h, start, x0]
                if engine == "S":
                    nc.scalar.mul(out=scores[:], in_=bank[:], mul=SCALE)
                else:
                    nc.vector.tensor_scalar_mul(out=scores[:], in0=bank[:], scalar1=SCALE)
                nc.sync.dma_start(out=out[0, h, start : start + CHUNK, x0:x1], in_=scores[:])

        for side in ("k", "q"):
            nc.vector.memset(w_plane[side][:].bitcast(I32), 0)

        load_features(nc.scalar, 0, "k", 0, 256)
        load_features(nc.scalar, 0, "k", 256, 512)
        load_scales("k")
        load_words("k")
        load_features(nc.sync, 0, "q", 0, 512)
        load_scales("q")
        load_words("q")
        load_features(nc.sync, 1, "k", 0, 512)
        load_features(nc.sync, 1, "q", 0, 512)

        regroup(nc.vector.tensor_copy, 0, "k", 0, 128)
        regroup(nc.vector.tensor_copy, 0, "k", 128, 256)
        quantise_features(0, "k", 0, 128)
        project(0, "k", 0, 128)
        round_projection(nc.scalar.copy, 0, "k", 0, 128)
        quantise_features(0, "k", 128, 256)
        project(0, "k", 128, 256)
        round_projection(nc.scalar.copy, 0, "k", 128, 256)
        regroup(nc.vector.tensor_copy, 0, "k", 256, 384)
        regroup(nc.vector.tensor_copy, 0, "k", 384, 512)
        quantise_features(0, "k", 256, 384)
        project(0, "k", 256, 384)
        round_projection(nc.scalar.copy, 0, "k", 256, 384)
        quantise_features(0, "k", 384, 512)
        project(0, "k", 384, 512)
        round_projection(nc.scalar.copy, 0, "k", 384, 512)
        regroup(nc.vector.tensor_copy, 0, "q", 0, 256)
        regroup(nc.vector.tensor_copy, 0, "q", 256, 512)
        quantise_features(0, "q", 0, 256)
        project(0, "q", 0, 256)
        round_projection(nc.scalar.copy, 0, "q", 0, 256)
        quantise_features(0, "q", 256, 512)
        project(0, "q", 256, 512)
        round_projection(nc.scalar.copy, 0, "q", 256, 512)
        quantise_projection(0, "k", 0, 256)
        regroup(nc.vector.tensor_copy, 1, "k", 0, 256)
        regroup(nc.vector.tensor_copy, 1, "k", 256, 512)
        quantise_features(1, "k", 0, 256)
        project(1, "k", 0, 256)
        round_projection(nc.scalar.copy, 1, "k", 0, 256)
        quantise_features(1, "k", 256, 512)
        project(1, "k", 256, 512)
        quantise_projection(0, "k", 256, 512)
        quantise_projection(0, "q", 0, 256)
        multiply(0, 0, 256)
        scale_and_store("S", 0, 0, 256)
        regroup(nc.vector.tensor_copy, 1, "q", 0, 256)
        quantise_projection(0, "q", 256, 512)
        multiply(0, 256, 512)
        quantise_features(1, "q", 0, 256)
        project(1, "q", 0, 256)
        regroup(nc.vector.tensor_copy, 1, "q", 256, 512)
        round_projection(nc.vector.tensor_copy, 1, "k", 256, 384)
        round_projection(nc.scalar.copy, 1, "k", 384, 512)
        quantise_projection(1, "k", 0, 256)
        quantise_features(1, "q", 256, 512)
        project(1, "q", 256, 512)
        round_projection(nc.scalar.copy, 1, "q", 0, 128)
        round_projection(nc.vector.tensor_copy, 1, "q", 128, 256)
        scale_and_store("S", 0, 256, 384)
        quantise_projection(1, "k", 256, 512)
        quantise_projection(1, "q", 0, 256)
        multiply(1, 0, 256)
        round_projection(nc.scalar.copy, 1, "q", 256, 512)
        scale_and_store("V", 0, 384, 512)
        quantise_projection(1, "q", 256, 384)
        multiply(1, 256, 384)
        scale_and_store("V", 1, 0, 128)
        quantise_projection(1, "q", 384, 512)
        scale_and_store("S", 1, 128, 256)
        multiply(1, 384, 512, 0, 256)
        multiply(1, 384, 512, 256, 512)
        scale_and_store("S", 1, 256, 384)
        scale_and_store("V", 1, 384, 512, 0, 256)
        scale_and_store("S", 1, 384, 512, 256, 512)
